import numpy as np
import ml_dtypes

BF16 = ml_dtypes.bfloat16


def bf(x):
    return np.asarray(x, np.float32).astype(BF16)


def f32(x):
    return np.asarray(x, np.float32)


def f64(x):
    return np.asarray(x).astype(np.float64)


def striped(idx):
    return np.tile(idx.reshape(-1, 16).T, (8, 1))


C, S, K, SET, H, N = 128, 256, 9, 8, 128, 1152


def setup_inputs():
    idx = np.concatenate([np.random.permutation(S)[:H] for _ in range(K)])
    return {"x": f32(np.random.standard_normal((C, S))), "w": f32(np.random.uniform(-1.0, 1.0, (C, K * SET))), "offs": striped(idx)}


def reference(x, w, offs):
    idx = offs[:16].T.reshape(-1)
    picked = f64(x)[:, idx].reshape(C, 1, K, H)
    wk = f64(w).reshape(C, K, SET).transpose(0, 2, 1)[:, :, :, None]
    return (picked * wk).reshape(C, SET * N)

@@ -1,0 +1,42 @@
+import concourse.mybir as mybir
+
+F32 = mybir.dt.float32
+U16 = mybir.dt.uint16
+MULT = mybir.AluOpType.mult
+COPY = mybir.ActivationFunctionType.Copy
+
+CHANNELS = 128
+PLACES = 256
+TAPS = 9
+SETS = 8
+PICKS = 128
+LIST = TAPS * PICKS
+OFFSETS_PER_COLUMN = 16
+
+
+def tile_capchmatch_kernel(tc, x, w, offs, out):
+    nc = tc.nc
+    with tc.tile_pool(name="held", bufs=1) as held:
+        offsets = held.tile([CHANNELS, LIST // OFFSETS_PER_COLUMN], U16, name="offsets")
+        nc.sync.dma_start(offsets[:], offs)
+        weights = held.tile([CHANNELS, TAPS * SETS], F32, name="weights")
+        nc.scalar.dma_start(weights[:], w)
+        feature_map = held.tile([CHANNELS, PLACES], F32, name="feature_map")
+        nc.sync.dma_start(feature_map[:], x)
+
+        spread = held.tile([CHANNELS, SETS * LIST], F32, name="spread")
+        votes = held.tile([CHANNELS, SETS * LIST], F32, name="votes")
+        by_tap = weights[:].rearrange("c (k e) -> c k e", e=SETS)
+        tap_columns = PICKS // OFFSETS_PER_COLUMN
+        for e in range(SETS):
+            whole_set = slice(e * LIST, (e + 1) * LIST)
+            nc.scalar.activation(
+                spread[:, whole_set].rearrange("c (k h) -> c k h", h=PICKS),
+                by_tap[:, :, e : e + 1].to_broadcast([CHANNELS, TAPS, PICKS]),
+                COPY,
+            )
+            for k in range(TAPS):
+                columns = slice(e * LIST + k * PICKS, e * LIST + (k + 1) * PICKS)
+                picked = feature_map[:].indirect(offsets[:, k * tap_columns : (k + 1) * tap_columns])
+                nc.vector.tensor_tensor(votes[:, columns], picked, spread[:, columns], MULT)
+            nc.sync.dma_start(out[:, whole_set], votes[:, whole_set])

@@ -12,6 +12,7 @@ SETS = 8
 PICKS = 128
 LIST = TAPS * PICKS
 OFFSETS_PER_COLUMN = 16
+PIECE = PLACES
 
 
 def tile_capchmatch_kernel(tc, x, w, offs, out):
@@ -27,7 +28,6 @@ def tile_capchmatch_kernel(tc, x, w, offs, out):
         spread = held.tile([CHANNELS, SETS * LIST], F32, name="spread")
         votes = held.tile([CHANNELS, SETS * LIST], F32, name="votes")
         by_tap = weights[:].rearrange("c (k e) -> c k e", e=SETS)
-        tap_columns = PICKS // OFFSETS_PER_COLUMN
         for e in range(SETS):
             whole_set = slice(e * LIST, (e + 1) * LIST)
             nc.scalar.activation(
@@ -35,8 +35,11 @@ def tile_capchmatch_kernel(tc, x, w, offs, out):
                 by_tap[:, :, e : e + 1].to_broadcast([CHANNELS, TAPS, PICKS]),
                 COPY,
             )
-            for k in range(TAPS):
-                columns = slice(e * LIST + k * PICKS, e * LIST + (k + 1) * PICKS)
-                picked = feature_map[:].indirect(offsets[:, k * tap_columns : (k + 1) * tap_columns])
+            for start in range(0, LIST, PIECE):
+                stop = min(start + PIECE, LIST)
+                columns = slice(e * LIST + start, e * LIST + stop)
+                picked = feature_map[:].indirect(
+                    offsets[:, start // OFFSETS_PER_COLUMN : stop // OFFSETS_PER_COLUMN]
+                )
                 nc.vector.tensor_tensor(votes[:, columns], picked, spread[:, columns], MULT)
             nc.sync.dma_start(out[:, whole_set], votes[:, whole_set])

@@ -42,4 +42,4 @@ def tile_capchmatch_kernel(tc, x, w, offs, out):
                     offsets[:, start // OFFSETS_PER_COLUMN : stop // OFFSETS_PER_COLUMN]
                 )
                 nc.vector.tensor_tensor(votes[:, columns], picked, spread[:, columns], MULT)
-            nc.sync.dma_start(out[:, whole_set], votes[:, whole_set])
+                nc.sync.dma_start(out[:, columns], votes[:, columns])

@@ -29,17 +29,20 @@ def tile_capchmatch_kernel(tc, x, w, offs, out):
         votes = held.tile([CHANNELS, SETS * LIST], F32, name="votes")
         by_tap = weights[:].rearrange("c (k e) -> c k e", e=SETS)
         for e in range(SETS):
-            whole_set = slice(e * LIST, (e + 1) * LIST)
-            nc.scalar.activation(
-                spread[:, whole_set].rearrange("c (k h) -> c k h", h=PICKS),
-                by_tap[:, :, e : e + 1].to_broadcast([CHANNELS, TAPS, PICKS]),
-                COPY,
-            )
             for start in range(0, LIST, PIECE):
                 stop = min(start + PIECE, LIST)
                 columns = slice(e * LIST + start, e * LIST + stop)
+                first_tap, end_tap = start // PICKS, stop // PICKS
+                nc.scalar.activation(
+                    spread[:, columns].rearrange("c (k h) -> c k h", h=PICKS),
+                    by_tap[:, first_tap:end_tap, e : e + 1].to_broadcast(
+                        [CHANNELS, end_tap - first_tap, PICKS]
+                    ),
+                    COPY,
+                )
                 picked = feature_map[:].indirect(
                     offsets[:, start // OFFSETS_PER_COLUMN : stop // OFFSETS_PER_COLUMN]
                 )
                 nc.vector.tensor_tensor(votes[:, columns], picked, spread[:, columns], MULT)
-                nc.sync.dma_start(out[:, columns], votes[:, columns])
+            whole_set = slice(e * LIST, (e + 1) * LIST)
+            nc.sync.dma_start(out[:, whole_set], votes[:, whole_set])

@@ -13,6 +13,7 @@ PICKS = 128
 LIST = TAPS * PICKS
 OFFSETS_PER_COLUMN = 16
 PIECE = PLACES
+STORE = 2 * PIECE
 
 
 def tile_capchmatch_kernel(tc, x, w, offs, out):
@@ -29,20 +30,22 @@ def tile_capchmatch_kernel(tc, x, w, offs, out):
         votes = held.tile([CHANNELS, SETS * LIST], F32, name="votes")
         by_tap = weights[:].rearrange("c (k e) -> c k e", e=SETS)
         for e in range(SETS):
-            for start in range(0, LIST, PIECE):
-                stop = min(start + PIECE, LIST)
-                columns = slice(e * LIST + start, e * LIST + stop)
-                first_tap, end_tap = start // PICKS, stop // PICKS
-                nc.scalar.activation(
-                    spread[:, columns].rearrange("c (k h) -> c k h", h=PICKS),
-                    by_tap[:, first_tap:end_tap, e : e + 1].to_broadcast(
-                        [CHANNELS, end_tap - first_tap, PICKS]
-                    ),
-                    COPY,
-                )
-                picked = feature_map[:].indirect(
-                    offsets[:, start // OFFSETS_PER_COLUMN : stop // OFFSETS_PER_COLUMN]
-                )
-                nc.vector.tensor_tensor(votes[:, columns], picked, spread[:, columns], MULT)
-            whole_set = slice(e * LIST, (e + 1) * LIST)
-            nc.sync.dma_start(out[:, whole_set], votes[:, whole_set])
+            for store_start in range(0, LIST, STORE):
+                store_stop = min(store_start + STORE, LIST)
+                for start in range(store_start, store_stop, PIECE):
+                    stop = min(start + PIECE, LIST)
+                    columns = slice(e * LIST + start, e * LIST + stop)
+                    first_tap, end_tap = start // PICKS, stop // PICKS
+                    nc.scalar.activation(
+                        spread[:, columns].rearrange("c (k h) -> c k h", h=PICKS),
+                        by_tap[:, first_tap:end_tap, e : e + 1].to_broadcast(
+                            [CHANNELS, end_tap - first_tap, PICKS]
+                        ),
+                        COPY,
+                    )
+                    picked = feature_map[:].indirect(
+                        offsets[:, start // OFFSETS_PER_COLUMN : stop // OFFSETS_PER_COLUMN]
+                    )
+                    nc.vector.tensor_tensor(votes[:, columns], picked, spread[:, columns], MULT)
+                stored = slice(e * LIST + store_start, e * LIST + store_stop)
+                nc.sync.dma_start(out[:, stored], votes[:, stored])

@@ -13,7 +13,7 @@ PICKS = 128
 LIST = TAPS * PICKS
 OFFSETS_PER_COLUMN = 16
 PIECE = PLACES
-STORE = 2 * PIECE
+LAST_STORES = 2 * PIECE
 
 
 def tile_capchmatch_kernel(tc, x, w, offs, out):
@@ -30,8 +30,9 @@ def tile_capchmatch_kernel(tc, x, w, offs, out):
         votes = held.tile([CHANNELS, SETS * LIST], F32, name="votes")
         by_tap = weights[:].rearrange("c (k e) -> c k e", e=SETS)
         for e in range(SETS):
-            for store_start in range(0, LIST, STORE):
-                store_stop = min(store_start + STORE, LIST)
+            store = LAST_STORES if e == SETS - 1 else LIST
+            for store_start in range(0, LIST, store):
+                store_stop = min(store_start + store, LIST)
                 for start in range(store_start, store_stop, PIECE):
                     stop = min(start + PIECE, LIST)
                     columns = slice(e * LIST + start, e * LIST + stop)

@@ -13,7 +13,7 @@ PICKS = 128
 LIST = TAPS * PICKS
 OFFSETS_PER_COLUMN = 16
 PIECE = PLACES
-LAST_STORES = 2 * PIECE
+LAST_STORES = PIECE
 
 
 def tile_capchmatch_kernel(tc, x, w, offs, out):

@@ -13,7 +13,16 @@ PICKS = 128
 LIST = TAPS * PICKS
 OFFSETS_PER_COLUMN = 16
 PIECE = PLACES
-LAST_STORES = PIECE
+
+
+def columns_of_a_store(e):
+    if e < SETS // 2:
+        return 2 * LIST
+    if e < SETS - 2:
+        return LIST
+    if e == SETS - 2:
+        return 2 * PIECE
+    return PIECE
 
 
 def tile_capchmatch_kernel(tc, x, w, offs, out):
@@ -29,24 +38,26 @@ def tile_capchmatch_kernel(tc, x, w, offs, out):
         spread = held.tile([CHANNELS, SETS * LIST], F32, name="spread")
         votes = held.tile([CHANNELS, SETS * LIST], F32, name="votes")
         by_tap = weights[:].rearrange("c (k e) -> c k e", e=SETS)
+        stored = 0
         for e in range(SETS):
-            store = LAST_STORES if e == SETS - 1 else LIST
-            for store_start in range(0, LIST, store):
-                store_stop = min(store_start + store, LIST)
-                for start in range(store_start, store_stop, PIECE):
-                    stop = min(start + PIECE, LIST)
-                    columns = slice(e * LIST + start, e * LIST + stop)
-                    first_tap, end_tap = start // PICKS, stop // PICKS
-                    nc.scalar.activation(
-                        spread[:, columns].rearrange("c (k h) -> c k h", h=PICKS),
-                        by_tap[:, first_tap:end_tap, e : e + 1].to_broadcast(
-                            [CHANNELS, end_tap - first_tap, PICKS]
-                        ),
-                        COPY,
-                    )
-                    picked = feature_map[:].indirect(
-                        offsets[:, start // OFFSETS_PER_COLUMN : stop // OFFSETS_PER_COLUMN]
-                    )
-                    nc.vector.tensor_tensor(votes[:, columns], picked, spread[:, columns], MULT)
-                stored = slice(e * LIST + store_start, e * LIST + store_stop)
-                nc.sync.dma_start(out[:, stored], votes[:, stored])
+            for start in range(0, LIST, PIECE):
+                stop = min(start + PIECE, LIST)
+                columns = slice(e * LIST + start, e * LIST + stop)
+                first_tap, end_tap = start // PICKS, stop // PICKS
+                nc.scalar.activation(
+                    spread[:, columns].rearrange("c (k h) -> c k h", h=PICKS),
+                    by_tap[:, first_tap:end_tap, e : e + 1].to_broadcast(
+                        [CHANNELS, end_tap - first_tap, PICKS]
+                    ),
+                    COPY,
+                )
+                picked = feature_map[:].indirect(
+                    offsets[:, start // OFFSETS_PER_COLUMN : stop // OFFSETS_PER_COLUMN]
+                )
+                nc.vector.tensor_tensor(votes[:, columns], picked, spread[:, columns], MULT)
+                finished = e * LIST + stop
+                full = finished - stored >= columns_of_a_store(e)
+                set_ends = stop == LIST and columns_of_a_store(e) <= LIST
+                if full or set_ends:
+                    nc.sync.dma_start(out[:, stored:finished], votes[:, stored:finished])
+                    stored = finished

@@ -18,9 +18,9 @@ PIECE = PLACES
 def columns_of_a_store(e):
     if e < SETS // 2:
         return 2 * LIST
-    if e < SETS - 2:
+    if e == SETS // 2:
         return LIST
-    if e == SETS - 2:
+    if e < SETS - 1:
         return 2 * PIECE
     return PIECE
 
@@ -40,8 +40,10 @@ def tile_capchmatch_kernel(tc, x, w, offs, out):
         by_tap = weights[:].rearrange("c (k e) -> c k e", e=SETS)
         stored = 0
         for e in range(SETS):
-            for start in range(0, LIST, PIECE):
-                stop = min(start + PIECE, LIST)
+            first_piece = PIECE if e == SETS - 1 else PICKS
+            ends = list(range(first_piece, LIST, PIECE)) + [LIST]
+            start = 0
+            for stop in ends:
                 columns = slice(e * LIST + start, e * LIST + stop)
                 first_tap, end_tap = start // PICKS, stop // PICKS
                 nc.scalar.activation(
@@ -61,3 +63,4 @@ def tile_capchmatch_kernel(tc, x, w, offs, out):
                 if full or set_ends:
                     nc.sync.dma_start(out[:, stored:finished], votes[:, stored:finished])
                     stored = finished
+                start = stop

@@ -29,11 +29,11 @@ def tile_capchmatch_kernel(tc, x, w, offs, out):
     nc = tc.nc
     with tc.tile_pool(name="held", bufs=1) as held:
         offsets = held.tile([CHANNELS, LIST // OFFSETS_PER_COLUMN], U16, name="offsets")
-        nc.sync.dma_start(offsets[:], offs)
         weights = held.tile([CHANNELS, TAPS * SETS], F32, name="weights")
         nc.scalar.dma_start(weights[:], w)
         feature_map = held.tile([CHANNELS, PLACES], F32, name="feature_map")
         nc.sync.dma_start(feature_map[:], x)
+        nc.sync.dma_start(offsets[:], offs)
 
         spread = held.tile([CHANNELS, SETS * LIST], F32, name="spread")
         votes = held.tile([CHANNELS, SETS * LIST], F32, name="votes")

@@ -30,9 +30,9 @@ def tile_capchmatch_kernel(tc, x, w, offs, out):
     with tc.tile_pool(name="held", bufs=1) as held:
         offsets = held.tile([CHANNELS, LIST // OFFSETS_PER_COLUMN], U16, name="offsets")
         weights = held.tile([CHANNELS, TAPS * SETS], F32, name="weights")
-        nc.scalar.dma_start(weights[:], w)
         feature_map = held.tile([CHANNELS, PLACES], F32, name="feature_map")
-        nc.sync.dma_start(feature_map[:], x)
+        nc.scalar.dma_start(feature_map[:], x)
+        nc.sync.dma_start(weights[:], w)
         nc.sync.dma_start(offsets[:], offs)
 
         spread = held.tile([CHANNELS, SETS * LIST], F32, name="spread")

import concourse.mybir as mybir

F32 = mybir.dt.float32
U16 = mybir.dt.uint16
MULT = mybir.AluOpType.mult
COPY = mybir.ActivationFunctionType.Copy

CHANNELS = 128
PLACES = 256
TAPS = 9
SETS = 8
PICKS = 128
LIST = TAPS * PICKS
OFFSETS_PER_COLUMN = 16
PIECE = PLACES


def columns_of_a_store(e):
    if e < SETS // 2:
        return 2 * LIST
    if e == SETS // 2:
        return LIST
    if e < SETS - 1:
        return 2 * PIECE
    return PIECE


def tile_capchmatch_kernel(tc, x, w, offs, out):
    nc = tc.nc
    with tc.tile_pool(name="held", bufs=1) as held:
        offsets = held.tile([CHANNELS, LIST // OFFSETS_PER_COLUMN], U16, name="offsets")
        weights = held.tile([CHANNELS, TAPS * SETS], F32, name="weights")
        feature_map = held.tile([CHANNELS, PLACES], F32, name="feature_map")
        nc.scalar.dma_start(feature_map[:], x)
        nc.sync.dma_start(weights[:], w)
        nc.sync.dma_start(offsets[:], offs)

        spread = held.tile([CHANNELS, SETS * LIST], F32, name="spread")
        votes = held.tile([CHANNELS, SETS * LIST], F32, name="votes")
        by_tap = weights[:].rearrange("c (k e) -> c k e", e=SETS)
        stored = 0
        for e in range(SETS):
            first_piece = PIECE if e == SETS - 1 else PICKS
            ends = list(range(first_piece, LIST, PIECE)) + [LIST]
            start = 0
            for stop in ends:
                columns = slice(e * LIST + start, e * LIST + stop)
                first_tap, end_tap = start // PICKS, stop // PICKS
                nc.scalar.activation(
                    spread[:, columns].rearrange("c (k h) -> c k h", h=PICKS),
                    by_tap[:, first_tap:end_tap, e : e + 1].to_broadcast(
                        [CHANNELS, end_tap - first_tap, PICKS]
                    ),
                    COPY,
                )
                picked = feature_map[:].indirect(
                    offsets[:, start // OFFSETS_PER_COLUMN : stop // OFFSETS_PER_COLUMN]
                )
                nc.vector.tensor_tensor(votes[:, columns], picked, spread[:, columns], MULT)
                finished = e * LIST + stop
                full = finished - stored >= columns_of_a_store(e)
                set_ends = stop == LIST and columns_of_a_store(e) <= LIST
                if full or set_ends:
                    nc.sync.dma_start(out[:, stored:finished], votes[:, stored:finished])
                    stored = finished
                start = stop
